import numpy as np
import ml_dtypes


def mxq(x, axis, fmt="e4m3"):
    dtype, down = {"e4m3": (ml_dtypes.float8_e4m3fn, 7), "e5m2": (ml_dtypes.float8_e5m2, 14)}[fmt]
    v = np.moveaxis(np.asarray(x, np.float32).astype(ml_dtypes.bfloat16).astype(np.float64), axis, -1)
    blocks = v.reshape(v.shape[:-1] + (-1, 32))
    amax = np.abs(blocks).max(-1, keepdims=True)
    byte = np.maximum(np.where(amax > 0, np.frexp(amax)[1] - 1 + 127, 0) - down, 1)
    scale = np.exp2(byte - 127.0)
    codes = (blocks / scale).astype(np.float32).astype(dtype).astype(np.float64)
    return np.moveaxis((codes * scale).reshape(v.shape), -1, axis)


WIDE = False


def mx_kscale(k):
    if not WIDE:
        return np.ones(k)
    levels = np.array([10, -10, 5, -5, 0])
    a = np.random.permutation(np.resize(levels, k // 512 * 4)).reshape(k // 512, 4)
    idx = np.arange(k)
    return np.exp2(a[idx // 512, idx % 128 // 32])


BF16 = ml_dtypes.bfloat16


def bf(x):
    return np.asarray(x, np.float32).astype(BF16)


def f64(x):
    return np.asarray(x).astype(np.float64)


E2M1 = np.array([0.0, 0.5, 1.0, 1.5, 2.0, 3.0, 4.0, 6.0, -0.0, -0.5, -1.0, -1.5, -2.0, -3.0, -4.0, -6.0])


def pack_weight(w, fmt):
    k, n = w.shape
    w = f64(bf(w)).reshape(k // 32, 32, n)
    amax = np.abs(w).max(1)
    if fmt == "e4m3":
        byte = np.frexp(amax)[1] - 1 + 127 - 7
    else:
        mant, ex = np.frexp(amax / 6.0)
        byte = np.where(mant > 0.5, ex, ex - 1) + 127
    byte = np.clip(np.where(amax > 0, byte, 1), 1, 254)
    scaled = (w * np.exp2(127.0 - byte)[:, None, :]).reshape(k, n).astype(np.float32)
    by_word = np.ascontiguousarray(scaled.reshape(k // 512, 128, 4, n).transpose(0, 1, 3, 2))
    if fmt == "e4m3":
        words = by_word.astype(ml_dtypes.float8_e4m3fn).view(np.uint8)
    else:
        c = by_word.astype(ml_dtypes.float4_e2m1fn).view(np.uint8) & 0xF
        words = c[..., 0::2] | (c[..., 1::2] << 4)
    return np.ascontiguousarray(words), np.ascontiguousarray(byte.astype(np.uint8).reshape(k // 512, 16, n))


def unpack_weight(words, scales, fmt):
    g, p, n, _ = words.shape
    if fmt == "e4m3":
        vals = np.ascontiguousarray(words).view(ml_dtypes.float8_e4m3fn).astype(np.float64)
    else:
        nib = np.empty((g, p, n, 4), np.uint8)
        nib[..., 0::2] = words & 0xF
        nib[..., 1::2] = words >> 4
        vals = E2M1[nib]
    vals = vals * np.repeat(np.exp2(scales.astype(np.float64) - 127.0), 8, axis=1)[..., None]
    return vals.transpose(0, 1, 3, 2).reshape(g * 512, n)

def pack4(w):
    words, scales = pack_weight(w, "e2m1")
    return words.reshape(words.shape[0], 128, -1), scales


def unpack4(words, scales):
    return unpack_weight(words.reshape(words.shape[0], 128, -1, 2), scales, "e2m1")


B, S, H, K, D, HID, WIN, QB = 1, 128, 8, 2, 128, 16384, 512, 512
T = B * S
NQKV = (H + 2 * K) * D


def rope(x, cos, sin):
    x1, x2 = np.split(x, 2, axis=-1)
    return np.concatenate([x1 * cos - x2 * sin, x2 * cos + x1 * sin], axis=-1)


def setup_inputs():
    s = mx_kscale(HID)
    ang = np.random.uniform(-np.pi, np.pi, (T, D // 2))
    hidden_states = bf(np.random.standard_normal((T, HID)) * s)
    w = np.random.standard_normal((NQKV, HID)) * 1.25 / np.sqrt(HID) / s[None, :]
    words, scales = pack4(np.ascontiguousarray(w.T))
    qkv_b = bf(np.random.standard_normal(NQKV) * 0.3)
    return {"hidden_states": hidden_states,
            "cos": bf(np.cos(ang)), "sin": bf(np.sin(ang)),
            "qkv_w_words": words, "qkv_w_scales": scales,
            "qkv_b": qkv_b}


def reference(hidden_states, cos, sin, qkv_w_words, qkv_w_scales, qkv_b):
    qkv = (mxq(f64(hidden_states), 1, "e4m3") @ unpack4(qkv_w_words, qkv_w_scales)) + f64(qkv_b)
    q = qkv[:, : H * D].reshape(B, S, H, D)
    k = qkv[:, H * D : (H + K) * D].reshape(B, S, K, D)
    v = qkv[:, (H + K) * D :].reshape(B, S, K, D)
    c = f64(cos).reshape(B, S, 1, D // 2)
    s = f64(sin).reshape(B, S, 1, D // 2)
    return rope(q, c, s), rope(k, c, s), v

@@ -1,0 +1,232 @@
+from contextlib import ExitStack
+
+import concourse.mybir as mybir
+from concourse.masks import make_identity
+
+F32 = mybir.dt.float32
+BF16 = mybir.dt.bfloat16
+I32 = mybir.dt.int32
+U32 = mybir.dt.uint32
+U8 = mybir.dt.uint8
+FP8X4 = mybir.dt.float8_e4m3fn_x4
+FP4X4 = mybir.dt.float4_e2m1fn_x4
+ADD = mybir.AluOpType.add
+SUBTRACT = mybir.AluOpType.subtract
+MULT = mybir.AluOpType.mult
+
+P = 128
+PACK = 4
+K_GROUP = P * PACK
+HID = 16384
+GROUPS = HID // K_GROUP
+SCALE_ROWS = K_GROUP // 32
+
+HEAD = 128
+HALF = HEAD // 2
+Q_COLS = 8 * HEAD
+K_COLS = 2 * HEAD
+V_COLS = 2 * HEAD
+ROPE_COLS = Q_COLS + K_COLS
+ALL_COLS = ROPE_COLS + V_COLS
+BANK_COLS = 512
+
+STRETCHES = 4
+GROUPS_PER_STRETCH = GROUPS // STRETCHES
+K_PER_STRETCH = GROUPS_PER_STRETCH * K_GROUP
+GROUPS_PER_BANK = 2
+SCALE_GROUPS_PER_DMA = 4
+V_GROUPS_PER_LOAD = 4
+
+FLOPS = 2 * P * HID * ALL_COLS
+
+
+def tile_starcoder2attention_pa_k_kernel(
+    tc, hidden_states, cos, sin, qkv_w_words, qkv_w_scales, qkv_b, out_0, out_1, out_2
+):
+    nc = tc.nc
+    with ExitStack() as ctx:
+        consts = ctx.enter_context(tc.tile_pool(name="consts", bufs=1))
+        x_pool = ctx.enter_context(tc.tile_pool(name="x_pool", bufs=2))
+        grouped_pool = ctx.enter_context(tc.tile_pool(name="grouped_pool", bufs=4))
+        rope_words_pool = ctx.enter_context(tc.tile_pool(name="rope_words_pool", bufs=GROUPS))
+        v_words_pool = ctx.enter_context(tc.tile_pool(name="v_words_pool", bufs=GROUPS // V_GROUPS_PER_LOAD))
+        acc_pool = ctx.enter_context(tc.psum_pool(name="acc_pool", bufs=1))
+        work_pool = ctx.enter_context(tc.psum_pool(name="work_pool", bufs=4))
+        ctx.enter_context(tc.manual_schedule())
+
+        identity = consts.tile([P, P], F32, name="identity")
+        make_identity(nc, identity[:])
+
+        w_scales = []
+        for c in range(STRETCHES):
+            plane = consts.tile([P, GROUPS_PER_STRETCH, ALL_COLS], U8, name="w_scales_%d" % c, align_bytes=64)
+            nc.vector.memset(plane[:].rearrange("p g n -> p (g n)").bitcast(I32), 0)
+            w_scales.append(plane)
+
+        ones = consts.tile([P, P], BF16, name="ones")
+        nc.vector.memset(ones[:], 1.0)
+        bias_rows = consts.tile([P, ALL_COLS], BF16, name="bias_rows")
+        nc.vector.memset(bias_rows[:], 0.0)
+        bias_all = consts.tile([P, ALL_COLS], F32, name="bias_all")
+        cos_bf = consts.tile([P, HALF], BF16, name="cos_bf")
+        sin_bf = consts.tile([P, HALF], BF16, name="sin_bf")
+        cos_f = consts.tile([P, HALF], F32, name="cos_f")
+        sin_f = consts.tile([P, HALF], F32, name="sin_f")
+
+        x_codes = []
+        x_scales = []
+        for c in range(STRETCHES):
+            x_codes.append(consts.tile([P, GROUPS_PER_STRETCH, P], U32, name="x_codes_%d" % c, align_bytes=64))
+            x_scales.append(consts.tile([P, GROUPS_PER_STRETCH, P], U8, name="x_scales_%d" % c, align_bytes=64))
+
+        rope_words = []
+        v_words = []
+
+        def load_stretch(c):
+            first_group = c * GROUPS_PER_STRETCH
+            x_raw = x_pool.tile([P, K_PER_STRETCH], BF16, name="x_raw")
+            nc.sync.dma_start(out=x_raw[:], in_=hidden_states[:, c * K_PER_STRETCH : (c + 1) * K_PER_STRETCH])
+            for part in range(0, GROUPS_PER_STRETCH, SCALE_GROUPS_PER_DMA):
+                for q in range(SCALE_ROWS // 2):
+                    partition = 32 * (q // 4) + q % 4
+                    rows = qkv_w_scales[
+                        first_group + part : first_group + part + SCALE_GROUPS_PER_DMA, q : SCALE_ROWS : SCALE_ROWS // 2, :
+                    ]
+                    nc.sync.dma_start(
+                        out=w_scales[c][partition : P : 64, part : part + SCALE_GROUPS_PER_DMA, :].bitcast(I32),
+                        in_=rows.rearrange("g q n -> q g n").bitcast(I32),
+                    )
+            for j in range(GROUPS_PER_STRETCH):
+                words = rope_words_pool.tile([P, 2 * ROPE_COLS], U8, name="rope_words", align_bytes=64)
+                nc.sync.dma_start(
+                    out=words[:].bitcast(I32), in_=qkv_w_words[first_group + j, :, 0 : 2 * ROPE_COLS].bitcast(I32)
+                )
+                rope_words.append(words)
+            return x_raw
+
+        def load_small_inputs():
+            nc.sync.dma_start(out=bias_rows[0:1, :], in_=qkv_b.unsqueeze(0))
+            nc.sync.dma_start(out=cos_bf[:], in_=cos)
+            nc.sync.dma_start(out=sin_bf[:], in_=sin)
+
+        def load_v_words():
+            for first_group in range(0, GROUPS, V_GROUPS_PER_LOAD):
+                words = v_words_pool.tile([P, V_GROUPS_PER_LOAD, 2 * V_COLS], U8, name="v_words", align_bytes=64)
+                rows = qkv_w_words[first_group : first_group + V_GROUPS_PER_LOAD, :, 2 * ROPE_COLS : 2 * ALL_COLS]
+                nc.sync.dma_start(out=words[:].bitcast(I32), in_=rows.rearrange("g p b -> p g b").bitcast(I32))
+                v_words.append(words)
+
+        def quantise_stretch(c, x_raw):
+            x_words = x_raw[:].bitcast(F32)
+            words_per_group = K_GROUP // 2
+            for first in range(0, GROUPS_PER_STRETCH, GROUPS_PER_BANK):
+                turned = work_pool.tile([P, GROUPS_PER_BANK, 2, P], F32, name="turned", tag="work")
+                for j in range(GROUPS_PER_BANK):
+                    start_word = (first + j) * words_per_group
+                    for u in range(2):
+                        nc.tensor.transpose(
+                            turned[:, j, u, :], x_words[:, start_word + u : start_word + words_per_group : 2], identity[:]
+                        )
+                grouped = grouped_pool.tile([P, GROUPS_PER_BANK, P, PACK], BF16, name="grouped", align_bytes=64)
+                nc.scalar.copy(out=grouped[:].bitcast(F32), in_=turned[:].rearrange("p j u r -> p j r u"))
+                nc.vector.quantize_mx(
+                    out=x_codes[c][:, first : first + GROUPS_PER_BANK, :].rearrange("p j r -> p (j r)").bitcast(FP8X4),
+                    scales=x_scales[c][:, first : first + GROUPS_PER_BANK, :].rearrange("p j r -> p (j r)"),
+                    in_=grouped[:].rearrange("p j r t -> p (j r t)"),
+                )
+
+        def mx_pass(acc, g, words, first_col, width):
+            c, j = divmod(g, GROUPS_PER_STRETCH)
+            nc.tensor.matmul_mx(
+                out=acc[:],
+                lhsT=x_codes[c][:, j, :].bitcast(FP8X4),
+                lhsT_scale=x_scales[c][:, j, :],
+                rhs=words.bitcast(FP4X4),
+                rhs_scale=w_scales[c][:, j, first_col : first_col + width],
+                start=(g == 0),
+                stop=(g == GROUPS - 1),
+            )
+
+        def spread_bias():
+            for first_col in range(0, ALL_COLS, BANK_COLS):
+                spread = work_pool.tile([P, BANK_COLS], F32, name="spread", tag="work")
+                nc.tensor.matmul(
+                    out=spread[:], lhsT=ones[:], rhs=bias_rows[:, first_col : first_col + BANK_COLS], start=True, stop=True
+                )
+                nc.scalar.copy(out=bias_all[:, first_col : first_col + BANK_COLS], in_=spread[:])
+            nc.vector.tensor_copy(out=cos_f[:], in_=cos_bf[:])
+            nc.vector.tensor_copy(out=sin_f[:], in_=sin_bf[:])
+
+        rope_sums = []
+        for first_col in range(0, Q_COLS, BANK_COLS):
+            rope_sums.append((acc_pool.tile([P, BANK_COLS], F32, name="q_sum_%d" % first_col), first_col, BANK_COLS))
+        for first_col in range(Q_COLS, ROPE_COLS, HEAD):
+            rope_sums.append((acc_pool.tile([P, HEAD], F32, name="k_sum_%d" % first_col), first_col, HEAD))
+
+        x_next = load_stretch(0)
+        load_small_inputs()
+        for c in range(STRETCHES):
+            x_raw = x_next
+            if c + 1 < STRETCHES:
+                x_next = load_stretch(c + 1)
+            else:
+                load_v_words()
+            quantise_stretch(c, x_raw)
+            for g in range(c * GROUPS_PER_STRETCH, (c + 1) * GROUPS_PER_STRETCH):
+                for acc, first_col, width in rope_sums:
+                    mx_pass(acc, g, rope_words[g][:, 2 * first_col : 2 * (first_col + width)], first_col, width)
+            if c == 0:
+                spread_bias()
+
+        rope_in = consts.tile([P, ROPE_COLS], F32, name="rope_in")
+        by_cos = consts.tile([P, ROPE_COLS], F32, name="by_cos")
+        by_sin = consts.tile([P, ROPE_COLS], F32, name="by_sin")
+        halves = ROPE_COLS // HALF
+        for acc, first_col, width in rope_sums:
+            nc.vector.tensor_tensor(
+                out=rope_in[:, first_col : first_col + width],
+                in0=acc[:],
+                in1=bias_all[:, first_col : first_col + width],
+                op=ADD,
+            )
+        nc.vector.tensor_tensor(
+            out=by_cos[:].rearrange("p (m d) -> p m d", d=HALF),
+            in0=rope_in[:].rearrange("p (m d) -> p m d", d=HALF),
+            in1=cos_f[:].unsqueeze(1).to_broadcast([P, halves, HALF]),
+            op=MULT,
+        )
+        nc.vector.tensor_tensor(
+            out=by_sin[:].rearrange("p (m d) -> p m d", d=HALF),
+            in0=rope_in[:].rearrange("p (m d) -> p m d", d=HALF),
+            in1=sin_f[:].unsqueeze(1).to_broadcast([P, halves, HALF]),
+            op=MULT,
+        )
+        out_q = out_0.rearrange("o s h d -> (o s) (h d)")
+        out_k = out_1.rearrange("o s h d -> (o s) (h d)")
+        out_v = out_2.rearrange("o s h d -> (o s) (h d)")
+        pieces = [(out_q[:, first_col : first_col + BANK_COLS], first_col, BANK_COLS) for first_col in range(0, Q_COLS, BANK_COLS)]
+        pieces.append((out_k, Q_COLS, K_COLS))
+        for dram, first_col, width in pieces:
+            c4 = by_cos[:, first_col : first_col + width].rearrange("p (h two d) -> p h two d", two=2, d=HALF)
+            s4 = by_sin[:, first_col : first_col + width].rearrange("p (h two d) -> p h two d", two=2, d=HALF)
+            nc.vector.tensor_tensor(out=c4[:, :, 0, :], in0=c4[:, :, 0, :], in1=s4[:, :, 1, :], op=SUBTRACT)
+            nc.vector.tensor_tensor(out=c4[:, :, 1, :], in0=c4[:, :, 1, :], in1=s4[:, :, 0, :], op=ADD)
+            nc.sync.dma_start(out=dram, in_=by_cos[:, first_col : first_col + width])
+
+        v_sums = []
+        for first_col in range(ROPE_COLS, ALL_COLS, HEAD):
+            v_sums.append((work_pool.tile([P, HEAD], F32, name="v_sum_%d" % first_col, tag="work"), first_col))
+        for g in range(GROUPS):
+            load, j = divmod(g, V_GROUPS_PER_LOAD)
+            for acc, first_col in v_sums:
+                first_byte = 2 * (first_col - ROPE_COLS)
+                mx_pass(acc, g, v_words[load][:, j, first_byte : first_byte + 2 * HEAD], first_col, HEAD)
+        v_out = consts.tile([P, V_COLS], F32, name="v_out")
+        for acc, first_col in v_sums:
+            nc.vector.tensor_tensor(
+                out=v_out[:, first_col - ROPE_COLS : first_col - ROPE_COLS + HEAD],
+                in0=acc[:],
+                in1=bias_all[:, first_col : first_col + HEAD],
+                op=ADD,
+            )
+        nc.sync.dma_start(out=out_v, in_=v_out[:])

@@ -157,6 +157,25 @@ def tile_starcoder2attention_pa_k_kernel(
             nc.vector.tensor_copy(out=cos_f[:], in_=cos_bf[:])
             nc.vector.tensor_copy(out=sin_f[:], in_=sin_bf[:])
 
+        by_cos = consts.tile([P, ROPE_COLS], F32, name="by_cos")
+        by_sin = consts.tile([P, ROPE_COLS], F32, name="by_sin")
+        bias_rot = consts.tile([P, ROPE_COLS], F32, name="bias_rot")
+
+        def rotate_bias():
+            halves = ROPE_COLS // HALF
+            for factor, product in ((cos_f, by_cos), (sin_f, by_sin)):
+                nc.vector.tensor_tensor(
+                    out=product[:].rearrange("p (m d) -> p m d", d=HALF),
+                    in0=bias_all[:, 0:ROPE_COLS].rearrange("p (m d) -> p m d", d=HALF),
+                    in1=factor[:].unsqueeze(1).to_broadcast([P, halves, HALF]),
+                    op=MULT,
+                )
+            c4 = by_cos[:].rearrange("p (h two d) -> p h two d", two=2, d=HALF)
+            s4 = by_sin[:].rearrange("p (h two d) -> p h two d", two=2, d=HALF)
+            r4 = bias_rot[:].rearrange("p (h two d) -> p h two d", two=2, d=HALF)
+            nc.vector.tensor_tensor(out=r4[:, :, 0, :], in0=c4[:, :, 0, :], in1=s4[:, :, 1, :], op=SUBTRACT)
+            nc.vector.tensor_tensor(out=r4[:, :, 1, :], in0=c4[:, :, 1, :], in1=s4[:, :, 0, :], op=ADD)
+
         rope_sums = []
         for first_col in range(0, Q_COLS, BANK_COLS):
             rope_sums.append((acc_pool.tile([P, BANK_COLS], F32, name="q_sum_%d" % first_col), first_col, BANK_COLS))
@@ -177,35 +196,37 @@ def tile_starcoder2attention_pa_k_kernel(
                     mx_pass(acc, g, rope_words[g][:, 2 * first_col : 2 * (first_col + width)], first_col, width)
             if c == 0:
                 spread_bias()
+            if c == 1:
+                rotate_bias()
 
-        rope_in = consts.tile([P, ROPE_COLS], F32, name="rope_in")
-        by_cos = consts.tile([P, ROPE_COLS], F32, name="by_cos")
-        by_sin = consts.tile([P, ROPE_COLS], F32, name="by_sin")
-        halves = ROPE_COLS // HALF
-        for acc, first_col, width in rope_sums:
-            nc.vector.tensor_tensor(
-                out=rope_in[:, first_col : first_col + width],
-                in0=acc[:],
-                in1=bias_all[:, first_col : first_col + width],
-                op=ADD,
-            )
-        nc.vector.tensor_tensor(
-            out=by_cos[:].rearrange("p (m d) -> p m d", d=HALF),
-            in0=rope_in[:].rearrange("p (m d) -> p m d", d=HALF),
-            in1=cos_f[:].unsqueeze(1).to_broadcast([P, halves, HALF]),
-            op=MULT,
-        )
-        nc.vector.tensor_tensor(
-            out=by_sin[:].rearrange("p (m d) -> p m d", d=HALF),
-            in0=rope_in[:].rearrange("p (m d) -> p m d", d=HALF),
-            in1=sin_f[:].unsqueeze(1).to_broadcast([P, halves, HALF]),
-            op=MULT,
-        )
         out_q = out_0.rearrange("o s h d -> (o s) (h d)")
         out_k = out_1.rearrange("o s h d -> (o s) (h d)")
         out_v = out_2.rearrange("o s h d -> (o s) (h d)")
         pieces = [(out_q[:, first_col : first_col + BANK_COLS], first_col, BANK_COLS) for first_col in range(0, Q_COLS, BANK_COLS)]
         pieces.append((out_k, Q_COLS, K_COLS))
+        for dram, piece_col, piece_width in pieces:
+            for acc, first_col, width in rope_sums:
+                if piece_col <= first_col < piece_col + piece_width:
+                    nc.vector.tensor_tensor(
+                        out=by_cos[:, first_col : first_col + width].rearrange("p (m d) -> p m d", d=HALF),
+                        in0=acc[:].rearrange("p (m d) -> p m d", d=HALF),
+                        in1=cos_f[:].unsqueeze(1).to_broadcast([P, width // HALF, HALF]),
+                        op=MULT,
+                    )
+            nc.gpsimd.tensor_tensor(
+                out=by_cos[:, piece_col : piece_col + piece_width],
+                in0=by_cos[:, piece_col : piece_col + piece_width],
+                in1=bias_rot[:, piece_col : piece_col + piece_width],
+                op=ADD,
+            )
+            for acc, first_col, width in rope_sums:
+                if piece_col <= first_col < piece_col + piece_width:
+                    nc.vector.tensor_tensor(
+                        out=by_sin[:, first_col : first_col + width].rearrange("p (m d) -> p m d", d=HALF),
+                        in0=acc[:].rearrange("p (m d) -> p m d", d=HALF),
+                        in1=sin_f[:].unsqueeze(1).to_broadcast([P, width // HALF, HALF]),
+                        op=MULT,
+                    )
         for dram, first_col, width in pieces:
             c4 = by_cos[:, first_col : first_col + width].rearrange("p (h two d) -> p h two d", two=2, d=HALF)
             s4 = by_sin[:, first_col : first_col + width].rearrange("p (h two d) -> p h two d", two=2, d=HALF)

@@ -35,7 +35,9 @@ GROUPS_PER_STRETCH = GROUPS // STRETCHES
 K_PER_STRETCH = GROUPS_PER_STRETCH * K_GROUP
 GROUPS_PER_BANK = 2
 SCALE_GROUPS_PER_DMA = 4
-V_GROUPS_PER_LOAD = 4
+WHOLE_ROW_GROUPS = GROUPS_PER_STRETCH
+V_LOADS = [4, 4, 4, 4, 4, 2, 1, 1]
+assert WHOLE_ROW_GROUPS + sum(V_LOADS) == GROUPS
 
 FLOPS = 2 * P * HID * ALL_COLS
 
@@ -48,8 +50,9 @@ def tile_starcoder2attention_pa_k_kernel(
         consts = ctx.enter_context(tc.tile_pool(name="consts", bufs=1))
         x_pool = ctx.enter_context(tc.tile_pool(name="x_pool", bufs=2))
         grouped_pool = ctx.enter_context(tc.tile_pool(name="grouped_pool", bufs=4))
-        rope_words_pool = ctx.enter_context(tc.tile_pool(name="rope_words_pool", bufs=GROUPS))
-        v_words_pool = ctx.enter_context(tc.tile_pool(name="v_words_pool", bufs=GROUPS // V_GROUPS_PER_LOAD))
+        whole_words_pool = ctx.enter_context(tc.tile_pool(name="whole_words_pool", bufs=WHOLE_ROW_GROUPS))
+        rope_words_pool = ctx.enter_context(tc.tile_pool(name="rope_words_pool", bufs=GROUPS - WHOLE_ROW_GROUPS))
+        v_words_pool = ctx.enter_context(tc.tile_pool(name="v_words_pool", bufs=1))
         acc_pool = ctx.enter_context(tc.psum_pool(name="acc_pool", bufs=1))
         work_pool = ctx.enter_context(tc.psum_pool(name="work_pool", bufs=4))
         ctx.enter_context(tc.manual_schedule())
@@ -96,11 +99,14 @@ def tile_starcoder2attention_pa_k_kernel(
                         out=w_scales[c][partition : P : 64, part : part + SCALE_GROUPS_PER_DMA, :].bitcast(I32),
                         in_=rows.rearrange("g q n -> q g n").bitcast(I32),
                     )
-            for j in range(GROUPS_PER_STRETCH):
-                words = rope_words_pool.tile([P, 2 * ROPE_COLS], U8, name="rope_words", align_bytes=64)
-                nc.sync.dma_start(
-                    out=words[:].bitcast(I32), in_=qkv_w_words[first_group + j, :, 0 : 2 * ROPE_COLS].bitcast(I32)
-                )
+            for g in range(first_group, first_group + GROUPS_PER_STRETCH):
+                if g < WHOLE_ROW_GROUPS:
+                    words = whole_words_pool.tile([P, 2 * ALL_COLS], U8, name="whole_words", align_bytes=64)
+                    nc.sync.dma_start(out=words[:].bitcast(I32), in_=qkv_w_words[g, :, :].bitcast(I32))
+                    v_words.append(words[:, 2 * ROPE_COLS : 2 * ALL_COLS])
+                else:
+                    words = rope_words_pool.tile([P, 2 * ROPE_COLS], U8, name="rope_words", align_bytes=64)
+                    nc.sync.dma_start(out=words[:].bitcast(I32), in_=qkv_w_words[g, :, 0 : 2 * ROPE_COLS].bitcast(I32))
                 rope_words.append(words)
             return x_raw
 
@@ -110,11 +116,14 @@ def tile_starcoder2attention_pa_k_kernel(
             nc.sync.dma_start(out=sin_bf[:], in_=sin)
 
         def load_v_words():
-            for first_group in range(0, GROUPS, V_GROUPS_PER_LOAD):
-                words = v_words_pool.tile([P, V_GROUPS_PER_LOAD, 2 * V_COLS], U8, name="v_words", align_bytes=64)
-                rows = qkv_w_words[first_group : first_group + V_GROUPS_PER_LOAD, :, 2 * ROPE_COLS : 2 * ALL_COLS]
+            first_group = WHOLE_ROW_GROUPS
+            for count in V_LOADS:
+                words = v_words_pool.tile([P, count, 2 * V_COLS], U8, name="v_words_%d" % first_group, align_bytes=64)
+                rows = qkv_w_words[first_group : first_group + count, :, 2 * ROPE_COLS : 2 * ALL_COLS]
                 nc.sync.dma_start(out=words[:].bitcast(I32), in_=rows.rearrange("g p b -> p g b").bitcast(I32))
-                v_words.append(words)
+                for j in range(count):
+                    v_words.append(words[:, j, :])
+                first_group += count
 
         def quantise_stretch(c, x_raw):
             x_words = x_raw[:].bitcast(F32)
@@ -135,16 +144,16 @@ def tile_starcoder2attention_pa_k_kernel(
                     in_=grouped[:].rearrange("p j r t -> p (j r t)"),
                 )
 
-        def mx_pass(acc, g, words, first_col, width):
+        def mx_pass(acc, g, words, first_col, width, first_g=0, last_g=GROUPS - 1):
             c, j = divmod(g, GROUPS_PER_STRETCH)
             nc.tensor.matmul_mx(
-                out=acc[:],
+                out=acc,
                 lhsT=x_codes[c][:, j, :].bitcast(FP8X4),
                 lhsT_scale=x_scales[c][:, j, :],
                 rhs=words.bitcast(FP4X4),
                 rhs_scale=w_scales[c][:, j, first_col : first_col + width],
-                start=(g == 0),
-                stop=(g == GROUPS - 1),
+                start=(g == first_g),
+                stop=(g == last_g),
             )
 
         def spread_bias():
@@ -176,6 +185,23 @@ def tile_starcoder2attention_pa_k_kernel(
             nc.vector.tensor_tensor(out=r4[:, :, 0, :], in0=c4[:, :, 0, :], in1=s4[:, :, 1, :], op=SUBTRACT)
             nc.vector.tensor_tensor(out=r4[:, :, 1, :], in0=c4[:, :, 1, :], in1=s4[:, :, 0, :], op=ADD)
 
+        v_part = consts.tile([P, V_COLS], F32, name="v_part")
+
+        def sum_early_v():
+            early = work_pool.tile([P, V_COLS], F32, name="early", tag="work")
+            for head_col in range(0, V_COLS, HEAD):
+                for g in range(WHOLE_ROW_GROUPS):
+                    mx_pass(
+                        early[:, head_col : head_col + HEAD],
+                        g,
+                        v_words[g][:, 2 * head_col : 2 * (head_col + HEAD)],
+                        ROPE_COLS + head_col,
+                        HEAD,
+                        0,
+                        WHOLE_ROW_GROUPS - 1,
+                    )
+            nc.vector.tensor_tensor(out=v_part[:], in0=early[:], in1=bias_all[:, ROPE_COLS:ALL_COLS], op=ADD)
+
         rope_sums = []
         for first_col in range(0, Q_COLS, BANK_COLS):
             rope_sums.append((acc_pool.tile([P, BANK_COLS], F32, name="q_sum_%d" % first_col), first_col, BANK_COLS))
@@ -193,9 +219,10 @@ def tile_starcoder2attention_pa_k_kernel(
             quantise_stretch(c, x_raw)
             for g in range(c * GROUPS_PER_STRETCH, (c + 1) * GROUPS_PER_STRETCH):
                 for acc, first_col, width in rope_sums:
-                    mx_pass(acc, g, rope_words[g][:, 2 * first_col : 2 * (first_col + width)], first_col, width)
+                    mx_pass(acc[:], g, rope_words[g][:, 2 * first_col : 2 * (first_col + width)], first_col, width)
             if c == 0:
                 spread_bias()
+                sum_early_v()
             if c == 1:
                 rotate_bias()
 
@@ -237,17 +264,16 @@ def tile_starcoder2attention_pa_k_kernel(
         v_sums = []
         for first_col in range(ROPE_COLS, ALL_COLS, HEAD):
             v_sums.append((work_pool.tile([P, HEAD], F32, name="v_sum_%d" % first_col, tag="work"), first_col))
-        for g in range(GROUPS):
-            load, j = divmod(g, V_GROUPS_PER_LOAD)
+        for g in range(WHOLE_ROW_GROUPS, GROUPS):
             for acc, first_col in v_sums:
                 first_byte = 2 * (first_col - ROPE_COLS)
-                mx_pass(acc, g, v_words[load][:, j, first_byte : first_byte + 2 * HEAD], first_col, HEAD)
+                mx_pass(acc[:], g, v_words[g][:, first_byte : first_byte + 2 * HEAD], first_col, HEAD, WHOLE_ROW_GROUPS)
         v_out = consts.tile([P, V_COLS], F32, name="v_out")
         for acc, first_col in v_sums:
             nc.vector.tensor_tensor(
                 out=v_out[:, first_col - ROPE_COLS : first_col - ROPE_COLS + HEAD],
                 in0=acc[:],
-                in1=bias_all[:, first_col : first_col + HEAD],
+                in1=v_part[:, first_col - ROPE_COLS : first_col - ROPE_COLS + HEAD],
                 op=ADD,
             )
         nc.sync.dma_start(out=out_v, in_=v_out[:])

from contextlib import ExitStack

import concourse.mybir as mybir
from concourse.masks import make_identity

F32 = mybir.dt.float32
BF16 = mybir.dt.bfloat16
I32 = mybir.dt.int32
U32 = mybir.dt.uint32
U8 = mybir.dt.uint8
FP8X4 = mybir.dt.float8_e4m3fn_x4
FP4X4 = mybir.dt.float4_e2m1fn_x4
ADD = mybir.AluOpType.add
SUBTRACT = mybir.AluOpType.subtract
MULT = mybir.AluOpType.mult

P = 128
PACK = 4
K_GROUP = P * PACK
HID = 16384
GROUPS = HID // K_GROUP
SCALE_ROWS = K_GROUP // 32

HEAD = 128
HALF = HEAD // 2
Q_COLS = 8 * HEAD
K_COLS = 2 * HEAD
V_COLS = 2 * HEAD
ROPE_COLS = Q_COLS + K_COLS
ALL_COLS = ROPE_COLS + V_COLS
BANK_COLS = 512

STRETCHES = 4
GROUPS_PER_STRETCH = GROUPS // STRETCHES
K_PER_STRETCH = GROUPS_PER_STRETCH * K_GROUP
GROUPS_PER_BANK = 2
SCALE_GROUPS_PER_DMA = 4
WHOLE_ROW_GROUPS = GROUPS_PER_STRETCH
V_LOADS = [4, 4, 4, 4, 4, 2, 1, 1]
assert WHOLE_ROW_GROUPS + sum(V_LOADS) == GROUPS

FLOPS = 2 * P * HID * ALL_COLS


def tile_starcoder2attention_pa_k_kernel(
    tc, hidden_states, cos, sin, qkv_w_words, qkv_w_scales, qkv_b, out_0, out_1, out_2
):
    nc = tc.nc
    with ExitStack() as ctx:
        consts = ctx.enter_context(tc.tile_pool(name="consts", bufs=1))
        x_pool = ctx.enter_context(tc.tile_pool(name="x_pool", bufs=2))
        grouped_pool = ctx.enter_context(tc.tile_pool(name="grouped_pool", bufs=4))
        whole_words_pool = ctx.enter_context(tc.tile_pool(name="whole_words_pool", bufs=WHOLE_ROW_GROUPS))
        rope_words_pool = ctx.enter_context(tc.tile_pool(name="rope_words_pool", bufs=GROUPS - WHOLE_ROW_GROUPS))
        v_words_pool = ctx.enter_context(tc.tile_pool(name="v_words_pool", bufs=1))
        acc_pool = ctx.enter_context(tc.psum_pool(name="acc_pool", bufs=1))
        work_pool = ctx.enter_context(tc.psum_pool(name="work_pool", bufs=4))
        ctx.enter_context(tc.manual_schedule())

        identity = consts.tile([P, P], F32, name="identity")
        make_identity(nc, identity[:])

        w_scales = []
        for c in range(STRETCHES):
            plane = consts.tile([P, GROUPS_PER_STRETCH, ALL_COLS], U8, name="w_scales_%d" % c, align_bytes=64)
            nc.vector.memset(plane[:].rearrange("p g n -> p (g n)").bitcast(I32), 0)
            w_scales.append(plane)

        ones = consts.tile([P, P], BF16, name="ones")
        nc.vector.memset(ones[:], 1.0)
        bias_rows = consts.tile([P, ALL_COLS], BF16, name="bias_rows")
        nc.vector.memset(bias_rows[:], 0.0)
        bias_all = consts.tile([P, ALL_COLS], F32, name="bias_all")
        cos_bf = consts.tile([P, HALF], BF16, name="cos_bf")
        sin_bf = consts.tile([P, HALF], BF16, name="sin_bf")
        cos_f = consts.tile([P, HALF], F32, name="cos_f")
        sin_f = consts.tile([P, HALF], F32, name="sin_f")

        x_codes = []
        x_scales = []
        for c in range(STRETCHES):
            x_codes.append(consts.tile([P, GROUPS_PER_STRETCH, P], U32, name="x_codes_%d" % c, align_bytes=64))
            x_scales.append(consts.tile([P, GROUPS_PER_STRETCH, P], U8, name="x_scales_%d" % c, align_bytes=64))

        rope_words = []
        v_words = []

        def load_stretch(c):
            first_group = c * GROUPS_PER_STRETCH
            x_raw = x_pool.tile([P, K_PER_STRETCH], BF16, name="x_raw")
            nc.sync.dma_start(out=x_raw[:], in_=hidden_states[:, c * K_PER_STRETCH : (c + 1) * K_PER_STRETCH])
            for part in range(0, GROUPS_PER_STRETCH, SCALE_GROUPS_PER_DMA):
                for q in range(SCALE_ROWS // 2):
                    partition = 32 * (q // 4) + q % 4
                    rows = qkv_w_scales[
                        first_group + part : first_group + part + SCALE_GROUPS_PER_DMA, q : SCALE_ROWS : SCALE_ROWS // 2, :
                    ]
                    nc.sync.dma_start(
                        out=w_scales[c][partition : P : 64, part : part + SCALE_GROUPS_PER_DMA, :].bitcast(I32),
                        in_=rows.rearrange("g q n -> q g n").bitcast(I32),
                    )
            for g in range(first_group, first_group + GROUPS_PER_STRETCH):
                if g < WHOLE_ROW_GROUPS:
                    words = whole_words_pool.tile([P, 2 * ALL_COLS], U8, name="whole_words", align_bytes=64)
                    nc.sync.dma_start(out=words[:].bitcast(I32), in_=qkv_w_words[g, :, :].bitcast(I32))
                    v_words.append(words[:, 2 * ROPE_COLS : 2 * ALL_COLS])
                else:
                    words = rope_words_pool.tile([P, 2 * ROPE_COLS], U8, name="rope_words", align_bytes=64)
                    nc.sync.dma_start(out=words[:].bitcast(I32), in_=qkv_w_words[g, :, 0 : 2 * ROPE_COLS].bitcast(I32))
                rope_words.append(words)
            return x_raw

        def load_small_inputs():
            nc.sync.dma_start(out=bias_rows[0:1, :], in_=qkv_b.unsqueeze(0))
            nc.sync.dma_start(out=cos_bf[:], in_=cos)
            nc.sync.dma_start(out=sin_bf[:], in_=sin)

        def load_v_words():
            first_group = WHOLE_ROW_GROUPS
            for count in V_LOADS:
                words = v_words_pool.tile([P, count, 2 * V_COLS], U8, name="v_words_%d" % first_group, align_bytes=64)
                rows = qkv_w_words[first_group : first_group + count, :, 2 * ROPE_COLS : 2 * ALL_COLS]
                nc.sync.dma_start(out=words[:].bitcast(I32), in_=rows.rearrange("g p b -> p g b").bitcast(I32))
                for j in range(count):
                    v_words.append(words[:, j, :])
                first_group += count

        def quantise_stretch(c, x_raw):
            x_words = x_raw[:].bitcast(F32)
            words_per_group = K_GROUP // 2
            for first in range(0, GROUPS_PER_STRETCH, GROUPS_PER_BANK):
                turned = work_pool.tile([P, GROUPS_PER_BANK, 2, P], F32, name="turned", tag="work")
                for j in range(GROUPS_PER_BANK):
                    start_word = (first + j) * words_per_group
                    for u in range(2):
                        nc.tensor.transpose(
                            turned[:, j, u, :], x_words[:, start_word + u : start_word + words_per_group : 2], identity[:]
                        )
                grouped = grouped_pool.tile([P, GROUPS_PER_BANK, P, PACK], BF16, name="grouped", align_bytes=64)
                nc.scalar.copy(out=grouped[:].bitcast(F32), in_=turned[:].rearrange("p j u r -> p j r u"))
                nc.vector.quantize_mx(
                    out=x_codes[c][:, first : first + GROUPS_PER_BANK, :].rearrange("p j r -> p (j r)").bitcast(FP8X4),
                    scales=x_scales[c][:, first : first + GROUPS_PER_BANK, :].rearrange("p j r -> p (j r)"),
                    in_=grouped[:].rearrange("p j r t -> p (j r t)"),
                )

        def mx_pass(acc, g, words, first_col, width, first_g=0, last_g=GROUPS - 1):
            c, j = divmod(g, GROUPS_PER_STRETCH)
            nc.tensor.matmul_mx(
                out=acc,
                lhsT=x_codes[c][:, j, :].bitcast(FP8X4),
                lhsT_scale=x_scales[c][:, j, :],
                rhs=words.bitcast(FP4X4),
                rhs_scale=w_scales[c][:, j, first_col : first_col + width],
                start=(g == first_g),
                stop=(g == last_g),
            )

        def spread_bias():
            for first_col in range(0, ALL_COLS, BANK_COLS):
                spread = work_pool.tile([P, BANK_COLS], F32, name="spread", tag="work")
                nc.tensor.matmul(
                    out=spread[:], lhsT=ones[:], rhs=bias_rows[:, first_col : first_col + BANK_COLS], start=True, stop=True
                )
                nc.scalar.copy(out=bias_all[:, first_col : first_col + BANK_COLS], in_=spread[:])
            nc.vector.tensor_copy(out=cos_f[:], in_=cos_bf[:])
            nc.vector.tensor_copy(out=sin_f[:], in_=sin_bf[:])

        by_cos = consts.tile([P, ROPE_COLS], F32, name="by_cos")
        by_sin = consts.tile([P, ROPE_COLS], F32, name="by_sin")
        bias_rot = consts.tile([P, ROPE_COLS], F32, name="bias_rot")

        def rotate_bias():
            halves = ROPE_COLS // HALF
            for factor, product in ((cos_f, by_cos), (sin_f, by_sin)):
                nc.vector.tensor_tensor(
                    out=product[:].rearrange("p (m d) -> p m d", d=HALF),
                    in0=bias_all[:, 0:ROPE_COLS].rearrange("p (m d) -> p m d", d=HALF),
                    in1=factor[:].unsqueeze(1).to_broadcast([P, halves, HALF]),
                    op=MULT,
                )
            c4 = by_cos[:].rearrange("p (h two d) -> p h two d", two=2, d=HALF)
            s4 = by_sin[:].rearrange("p (h two d) -> p h two d", two=2, d=HALF)
            r4 = bias_rot[:].rearrange("p (h two d) -> p h two d", two=2, d=HALF)
            nc.vector.tensor_tensor(out=r4[:, :, 0, :], in0=c4[:, :, 0, :], in1=s4[:, :, 1, :], op=SUBTRACT)
            nc.vector.tensor_tensor(out=r4[:, :, 1, :], in0=c4[:, :, 1, :], in1=s4[:, :, 0, :], op=ADD)

        v_part = consts.tile([P, V_COLS], F32, name="v_part")

        def sum_early_v():
            early = work_pool.tile([P, V_COLS], F32, name="early", tag="work")
            for head_col in range(0, V_COLS, HEAD):
                for g in range(WHOLE_ROW_GROUPS):
                    mx_pass(
                        early[:, head_col : head_col + HEAD],
                        g,
                        v_words[g][:, 2 * head_col : 2 * (head_col + HEAD)],
                        ROPE_COLS + head_col,
                        HEAD,
                        0,
                        WHOLE_ROW_GROUPS - 1,
                    )
            nc.vector.tensor_tensor(out=v_part[:], in0=early[:], in1=bias_all[:, ROPE_COLS:ALL_COLS], op=ADD)

        rope_sums = []
        for first_col in range(0, Q_COLS, BANK_COLS):
            rope_sums.append((acc_pool.tile([P, BANK_COLS], F32, name="q_sum_%d" % first_col), first_col, BANK_COLS))
        for first_col in range(Q_COLS, ROPE_COLS, HEAD):
            rope_sums.append((acc_pool.tile([P, HEAD], F32, name="k_sum_%d" % first_col), first_col, HEAD))

        x_next = load_stretch(0)
        load_small_inputs()
        for c in range(STRETCHES):
            x_raw = x_next
            if c + 1 < STRETCHES:
                x_next = load_stretch(c + 1)
            else:
                load_v_words()
            quantise_stretch(c, x_raw)
            for g in range(c * GROUPS_PER_STRETCH, (c + 1) * GROUPS_PER_STRETCH):
                for acc, first_col, width in rope_sums:
                    mx_pass(acc[:], g, rope_words[g][:, 2 * first_col : 2 * (first_col + width)], first_col, width)
            if c == 0:
                spread_bias()
                sum_early_v()
            if c == 1:
                rotate_bias()

        out_q = out_0.rearrange("o s h d -> (o s) (h d)")
        out_k = out_1.rearrange("o s h d -> (o s) (h d)")
        out_v = out_2.rearrange("o s h d -> (o s) (h d)")
        pieces = [(out_q[:, first_col : first_col + BANK_COLS], first_col, BANK_COLS) for first_col in range(0, Q_COLS, BANK_COLS)]
        pieces.append((out_k, Q_COLS, K_COLS))
        for dram, piece_col, piece_width in pieces:
            for acc, first_col, width in rope_sums:
                if piece_col <= first_col < piece_col + piece_width:
                    nc.vector.tensor_tensor(
                        out=by_cos[:, first_col : first_col + width].rearrange("p (m d) -> p m d", d=HALF),
                        in0=acc[:].rearrange("p (m d) -> p m d", d=HALF),
                        in1=cos_f[:].unsqueeze(1).to_broadcast([P, width // HALF, HALF]),
                        op=MULT,
                    )
            nc.gpsimd.tensor_tensor(
                out=by_cos[:, piece_col : piece_col + piece_width],
                in0=by_cos[:, piece_col : piece_col + piece_width],
                in1=bias_rot[:, piece_col : piece_col + piece_width],
                op=ADD,
            )
            for acc, first_col, width in rope_sums:
                if piece_col <= first_col < piece_col + piece_width:
                    nc.vector.tensor_tensor(
                        out=by_sin[:, first_col : first_col + width].rearrange("p (m d) -> p m d", d=HALF),
                        in0=acc[:].rearrange("p (m d) -> p m d", d=HALF),
                        in1=sin_f[:].unsqueeze(1).to_broadcast([P, width // HALF, HALF]),
                        op=MULT,
                    )
        for dram, first_col, width in pieces:
            c4 = by_cos[:, first_col : first_col + width].rearrange("p (h two d) -> p h two d", two=2, d=HALF)
            s4 = by_sin[:, first_col : first_col + width].rearrange("p (h two d) -> p h two d", two=2, d=HALF)
            nc.vector.tensor_tensor(out=c4[:, :, 0, :], in0=c4[:, :, 0, :], in1=s4[:, :, 1, :], op=SUBTRACT)
            nc.vector.tensor_tensor(out=c4[:, :, 1, :], in0=c4[:, :, 1, :], in1=s4[:, :, 0, :], op=ADD)
            nc.sync.dma_start(out=dram, in_=by_cos[:, first_col : first_col + width])

        v_sums = []
        for first_col in range(ROPE_COLS, ALL_COLS, HEAD):
            v_sums.append((work_pool.tile([P, HEAD], F32, name="v_sum_%d" % first_col, tag="work"), first_col))
        for g in range(WHOLE_ROW_GROUPS, GROUPS):
            for acc, first_col in v_sums:
                first_byte = 2 * (first_col - ROPE_COLS)
                mx_pass(acc[:], g, v_words[g][:, first_byte : first_byte + 2 * HEAD], first_col, HEAD, WHOLE_ROW_GROUPS)
        v_out = consts.tile([P, V_COLS], F32, name="v_out")
        for acc, first_col in v_sums:
            nc.vector.tensor_tensor(
                out=v_out[:, first_col - ROPE_COLS : first_col - ROPE_COLS + HEAD],
                in0=acc[:],
                in1=v_part[:, first_col - ROPE_COLS : first_col - ROPE_COLS + HEAD],
                op=ADD,
            )
        nc.sync.dma_start(out=out_v, in_=v_out[:])
